import numpy as np
import ml_dtypes


def mxq(x, axis, fmt="e4m3"):
    dtype, down = {"e4m3": (ml_dtypes.float8_e4m3fn, 7), "e5m2": (ml_dtypes.float8_e5m2, 14)}[fmt]
    v = np.moveaxis(np.asarray(x, np.float32).astype(ml_dtypes.bfloat16).astype(np.float64), axis, -1)
    blocks = v.reshape(v.shape[:-1] + (-1, 32))
    amax = np.abs(blocks).max(-1, keepdims=True)
    byte = np.maximum(np.where(amax > 0, np.frexp(amax)[1] - 1 + 127, 0) - down, 1)
    scale = np.exp2(byte - 127.0)
    codes = (blocks / scale).astype(np.float32).astype(dtype).astype(np.float64)
    return np.moveaxis((codes * scale).reshape(v.shape), -1, axis)


WIDE = False


def mx_kscale(k):
    if not WIDE:
        return np.ones(k)
    levels = np.array([18, -18])
    if k % 512:
        return np.exp2(np.random.permutation(np.resize(levels, k // 32))).repeat(32)
    a = np.empty((k // 512, 16))
    for p in range(k // 512):
        a[p, :8] = np.random.permutation(np.resize(levels, 8))
        for g in range(8):
            far = levels[np.abs(levels - a[p, g]) >= 10]
            a[p, g + 8] = far[np.random.randint(len(far))]
    return np.exp2(a.ravel()).repeat(32)


BF16 = ml_dtypes.bfloat16


def bf(x):
    return np.asarray(x, np.float32).astype(BF16)


def f64(x):
    return np.asarray(x).astype(np.float64)


B, SS, SM, SL, N, D = 1, 512, 1024, 1536, 512, 512
T = SS + SM + SL
EPS = 1e-5


def setup_inputs():
    sl = mx_kscale(SL)
    s = np.concatenate([sl[:SS + SM], sl])[None, :, None]
    u = mx_kscale(3 * D)
    x0 = bf(np.random.standard_normal((B, T, N)))
    gamma = bf(1.0 + 0.1 * np.random.standard_normal(N))
    beta0 = bf(0.1 * np.random.standard_normal(N))
    d = {"x": bf(f64(x0) * s), "gamma": gamma, "beta": bf(f64(beta0) * np.min(sl))}
    for c in ("s", "m", "l"):
        w0 = bf(np.random.standard_normal((N, 3 * D)) * 1.5 / np.sqrt(N))
        d["Wqkv_" + c] = bf(f64(w0) / u)
        d["bqkv_" + c] = bf(0.1 * np.random.standard_normal(3 * D))
    xf = f64(x0)
    var = np.square(xf - xf.mean(-1, keepdims=True)).mean(-1, keepdims=True)
    d["rstd"] = np.asarray(1.0 / np.sqrt(var + EPS), np.float32)
    d["grad_out"] = bf(np.random.standard_normal((B, T, 3 * D))
                       * np.exp2(np.random.randint(-6, 1, (B, T, 1))) / s * u)
    return d


def back_rows(g, W):
    return mxq(g, 1, "e5m2") @ mxq(f64(W), 1, "e4m3").T


def reference(x, gamma, beta, Wqkv_s, bqkv_s, Wqkv_m, bqkv_m, Wqkv_l, bqkv_l, rstd, grad_out):
    xf = f64(x)[0]
    r = f64(rstd)[0]
    g = f64(grad_out)[0]
    ga = f64(gamma)
    xhat = (xf - xf.mean(-1, keepdims=True)) * r
    g_l = g[SS + SM:T]
    dh = np.concatenate([back_rows(g[:SS], Wqkv_s),
                         back_rows(g[SS:SS + SM], Wqkv_m),
                         back_rows(g_l, Wqkv_l)], axis=0)
    dxhat = dh * ga
    dx = r * (dxhat - dxhat.mean(-1, keepdims=True) - xhat * (dxhat * xhat).mean(-1, keepdims=True))
    h_l = xhat[SS + SM:T] * ga + f64(beta)
    dw = mxq(h_l, 0, "e4m3").T @ mxq(g_l, 0, "e5m2")
    return dx[None], dw

@@ -1,0 +1,380 @@
+from contextlib import ExitStack
+
+import concourse.mybir as mybir
+from concourse.masks import make_identity
+
+T, N, F = 3072, 512, 1536
+FLOPS = 2 * T * N * F + 2 * 1536 * N * F
+BYTES = 2 * (T * N + 2 * N + 3 * N * F + T * F) + 4 * (T + T * N + N * F)
+
+F32 = mybir.dt.float32
+BF16 = mybir.dt.bfloat16
+U32 = mybir.dt.uint32
+U8 = mybir.dt.uint8
+E4M3 = mybir.dt.float8_e4m3fn_x4
+E5M2 = mybir.dt.float8_e5m2_x4
+ALU = mybir.AluOpType
+IDENT = mybir.ActivationFunctionType.Identity
+
+P = 128
+PACK = 4
+KP = P * PACK
+PASSES = F // KP
+GROUPS = [3, 4, 5, 1, 2, 0]
+L_GROUPS = 3
+STEPS = len(GROUPS) * PACK
+
+PLAN = {
+    0: [("U", 1, 0), ("U", 1, 1), ("H", 0, 0)],
+    1: [("U", 1, 2), ("H", 0, 1), ("M", 1)],
+    2: [("H", 0, 2), ("I", 1, 0, 0), ("I", 1, 0, 1), ("X", 1)],
+    3: [("U", 2, 0), ("H", 1, 0)],
+    4: [("U", 2, 1), ("H", 1, 1)],
+    5: [("U", 2, 2), ("H", 1, 2), ("I", 2, 0, 0), ("M", 2)],
+    6: [("W", 1, 0), ("W", 1, 1), ("X", 2)],
+    7: [("U", 3, 0), ("W", 1, 2)],
+    8: [("U", 3, 1), ("H", 2, 0)],
+    9: [("U", 3, 2), ("H", 2, 1)],
+    10: [("H", 2, 2), ("I", 2, 0, 1), ("I", 1, 1, 0)],
+    11: [("U", 4, 0), ("I", 1, 1, 1)],
+    12: [("U", 4, 1), ("I", 2, 1, 0)],
+    13: [("U", 4, 2), ("I", 2, 1, 1), ("O", 0, 0)],
+    14: [("W", 2, 0), ("W", 2, 1), ("O", 1, 0)],
+    15: [("U", 5, 0), ("W", 2, 2), ("O", 2, 0)],
+    16: [("U", 5, 1), ("I", 1, 2, 0), ("O", 3, 0)],
+    17: [("U", 5, 2), ("I", 1, 2, 1), ("O", 0, 1)],
+    18: [("I", 2, 2, 0), ("I", 2, 2, 1), ("O", 1, 1)],
+    19: [("O", 2, 1), ("O", 3, 1)],
+    21: [("O", 0, 2), ("O", 1, 2)],
+    22: [("O", 2, 2), ("O", 3, 2)],
+}
+LOADS = {0: [("g", 2)], 1: [("x", 2), ("w", 1)], 3: [("g", 3)], 6: [("x", 3)], 7: [("g", 4)],
+         9: [("w", 2)], 10: [("x", 4)], 11: [("g", 5)], 14: [("x", 5)]}
+
+
+def tile_multiscalesattn_pa_v_kernel(
+    tc, x, gamma, beta, w_s, b_s, w_m, b_m, w_l, b_l, rstd, grad_out, out_0, out_1
+):
+    nc = tc.nc
+    weights = [w_l, w_m, w_s]
+    weight_of = [0, 0, 0, 1, 1, 2]
+    x_rows = x.rearrange("b (g p j) n -> (b g) p j n", p=P, j=PACK)
+    g_rows = grad_out.rearrange("b (g p j) f -> (b g) p j f", p=P, j=PACK)
+    dx_rows = out_0.rearrange("b (g p j) n -> (b g) p j n", p=P, j=PACK)
+
+    with ExitStack() as ctx:
+        sb = ctx.enter_context(tc.tile_pool(name="sb", bufs=1))
+        ps = ctx.enter_context(tc.psum_pool(name="ps", bufs=1))
+        ctx.enter_context(tc.manual_schedule())
+
+        g_raw, w_raw, x_raw = {}, {}, {}
+        codes = {}
+        xhat, neg_mean, h_t, work, stats, acc = {}, {}, {}, {}, {}, {}
+        staged = {}
+
+        def load_g(i):
+            tag = "g%d" % (i if i < 5 else 3)
+            t = sb.tile([P, PACK, F], BF16, name=tag)
+            nc.sync.dma_start(out=t[:], in_=g_rows[GROUPS[i]])
+            for c in range(PASSES):
+                g_raw[i, c] = t[:, :, c * KP : (c + 1) * KP]
+
+        def load_w(k):
+            for c in range(PASSES):
+                t = sb.tile([P, PACK, KP], BF16, name="w0_%d" % c)
+                nc.sync.dma_start(out=t[:], in_=weights[k].rearrange("(c p) f -> p c f", p=P)[:, :, c * KP : (c + 1) * KP])
+                w_raw[k, c] = t[:]
+
+        def load_x(i):
+            t = sb.tile([P, PACK, N], BF16, name="x", bufs=3)
+            nc.sync.dma_start(out=t[:], in_=x_rows[GROUPS[i]])
+            x_raw[i] = t
+
+        def turn(src, key):
+            words = src.bitcast(F32)
+            dst = sb.tile([P, PACK, P, 2], F32, name="turned", bufs=5, align_bytes=64)
+            for half in range(2):
+                bank = ps.tile([P, 2, 2, P], F32, name="tbank", bufs=4)
+                for a in range(2):
+                    for u in range(2):
+                        nc.tensor.transpose(bank[:, a, u, :], words[:, 2 * half + a, u : 2 * P : 2], ident[:])
+                nc.scalar.copy(out=dst[:, 2 * half : 2 * half + 2], in_=bank[:].rearrange("p a u r -> p a r u"))
+            staged[key] = dst[:].rearrange("p a r u -> p (a r u)").bitcast(BF16)
+
+        def quantize(key, fmt, tag, bufs):
+            cw = sb.tile([P, KP], U32, name=tag + "c", bufs=bufs, align_bytes=64)
+            cs = sb.tile([P, KP], U8, name=tag + "s", bufs=bufs, align_bytes=64)
+            nc.vector.quantize_mx(out=cw[:].bitcast(fmt), scales=cs[:], in_=staged[key])
+            codes[key] = (cw, cs)
+
+        def quantize_staged(key):
+            if key[0] == "g":
+                quantize(key, E5M2, "gf", 7)
+            elif key[0] == "w":
+                quantize(key, E4M3, "wf", 9)
+            elif key[0] == "t":
+                quantize(key, E5M2, "gt%d_%d" % (key[1], key[2] % 2 if key[1] else key[2]), 1)
+            else:
+                quantize(key, E4M3, "ht", 3)
+
+        def interleave(i, c, half, halves, engine):
+            key = ("t", i, c)
+            if half == 0:
+                dst = sb.tile([P, KP, PACK], BF16, name="woven", bufs=3, align_bytes=64)
+                work[key] = dst
+                staged[key] = dst[:].rearrange("p f t -> p (f t)")
+            width = KP // halves
+            cols = slice(half * width, (half + 1) * width)
+            src = g_raw[i, c][:, :, cols].rearrange("p t (c i) -> p c t i", i=4)
+            out = work[key][:, cols, :].rearrange("p (c i) t -> p c t i", i=4)
+            if engine == "V":
+                nc.vector.tensor_copy(out=out, in_=src)
+            else:
+                nc.scalar.copy(out=out, in_=src)
+
+        def row_means(i, js):
+            if i not in neg_mean:
+                neg_mean[i] = sb.tile([P, PACK], F32, name="negmean", bufs=3)
+            for j in js:
+                junk = sb.tile([P, N], BF16, name="mjunk", bufs=2)
+                nc.scalar.activation(out=junk[:], in_=x_raw[i][:, j, :], func=IDENT, scale=-1.0 / N,
+                                     accum_out=neg_mean[i][:, j : j + 1])
+
+        def row_means_v(i):
+            neg_mean[i] = sb.tile([P, PACK], F32, name="negmean", bufs=3)
+            for j in range(PACK):
+                junk = sb.tile([P, N], BF16, name="mjunk", bufs=2)
+                nc.vector.tensor_scalar(out=junk[:], in0=x_raw[i][:, j, :], scalar1=-1.0 / N, scalar2=None,
+                                        op0=ALU.mult, op1=ALU.add, accum_out=neg_mean[i][:, j : j + 1])
+
+        def normalise(i):
+            for j in range(PACK):
+                t = sb.tile([P, N], F32, name="xhat", bufs=8)
+                nc.vector.tensor_scalar(out=t[:], in0=x_raw[i][:, j, :], scalar1=neg_mean[i][:, j : j + 1],
+                                        scalar2=r[:, GROUPS[i], j : j + 1], op0=ALU.add, op1=ALU.mult)
+                xhat[i, j] = t
+
+        def h_columns(i, c):
+            bank = ps.tile([P, 2, 2, P], F32, name="tbank", bufs=4)
+            for j in range(PACK):
+                nc.tensor.transpose(bank[:, j // 2, j % 2, :], xhat[i, j][:, c * P : (c + 1) * P], ident[:])
+            t = sb.tile([P, 2, P, 2], BF16, name="hT", bufs=4)
+            nc.scalar.activation(out=t[:], in_=bank[:].rearrange("n u e p -> n u p e"), func=IDENT,
+                                 scale=gb[:, c : c + 1], bias=gb[:, PACK + c : PACK + c + 1])
+            h_t[i, c] = t[:].rearrange("n u p e -> n u (p e)").bitcast(F32)
+
+        def h_rows(i, half):
+            key = ("h", i)
+            if half == 0:
+                dst = sb.tile([P, PACK, P, 2], F32, name="hrows", bufs=1, align_bytes=64)
+                work[key] = dst
+                staged[key] = dst[:].rearrange("p a r u -> p (a r u)").bitcast(BF16)
+            bank = ps.tile([P, 2, 2, P], F32, name="tbank", bufs=4)
+            for a in range(2):
+                for u in range(2):
+                    nc.tensor.transpose(bank[:, a, u, :], h_t[i, 2 * half + a][:, u, :], ident[:])
+            nc.scalar.copy(out=work[key][:, 2 * half : 2 * half + 2], in_=bank[:].rearrange("p a u r -> p a r u"))
+
+        def product(bank, stat, stat_fmt, cols, mov, mov_fmt):
+            for c in range(PASSES):
+                nc.tensor.matmul_mx(
+                    out=bank[:],
+                    lhsT=stat[c][0][:, cols].bitcast(stat_fmt), lhsT_scale=stat[c][1][:, cols],
+                    rhs=mov[c][0][:].bitcast(mov_fmt), rhs_scale=mov[c][1][:],
+                    start=(c == 0), stop=(c == PASSES - 1),
+                )
+
+        def dh_product(t):
+            i, j = divmod(t, PACK)
+            bank = ps.tile([P, N], F32, name="dh", bufs=2)
+            product(bank, [codes["g", i, c] for c in range(PASSES)], E5M2, slice(j * P, (j + 1) * P),
+                    [codes["w", weight_of[i], c] for c in range(PASSES)], E4M3)
+            acc[t] = bank
+
+        def dw_product(m, c):
+            if 2 * c + m // 2 >= 3:
+                bank = ps.tile([P, KP], F32, name="tbank", bufs=4)
+            else:
+                bank = ps.tile([P, KP], F32, name="dw", bufs=2)
+            product(bank, [codes["h", i] for i in range(L_GROUPS)], E4M3, slice(m * P, (m + 1) * P),
+                    [codes["t", i, c] for i in range(L_GROUPS)], E5M2)
+            acc[m, c] = bank
+
+        def dw_store(m, c):
+            t = sb.tile([P, KP], F32, name="dwout", bufs=4)
+            nc.scalar.copy(out=t[:], in_=acc[m, c][:])
+            nc.sync.dma_start(out=out_1[m * P : (m + 1) * P, c * KP : (c + 1) * KP], in_=t[:])
+
+        def scale_rows(t):
+            i, j = divmod(t, PACK)
+            work[t] = sb.tile([P, N], F32, name="row", bufs=7)
+            stats[t] = sb.tile([P, 8], F32, name="stats", bufs=7)
+            nc.vector.scalar_tensor_tensor(out=work[t][:], in0=acc[t][:], scalar=r_over_n[:, GROUPS[i], j : j + 1],
+                                           in1=gamma_rows[:], op0=ALU.mult, op1=ALU.mult,
+                                           accum_out=stats[t][:, 0:1] if i >= L_GROUPS else None)
+
+        def row_mean_d(t):
+            if t // PACK >= L_GROUPS:
+                nc.vector.tensor_scalar(out=stats[t][:, 1:2], in0=stats[t][:, 0:1], scalar1=1.0 / N, scalar2=None,
+                                        op0=ALU.mult)
+
+        def project(t):
+            i, j = divmod(t, PACK)
+            junk = sb.tile([P, N], F32, name="pjunk", bufs=1)
+            if i < L_GROUPS:
+                nc.vector.scalar_tensor_tensor(out=junk[:], in0=work[t][:], scalar=-1.0 / N, in1=xhat[i, j][:],
+                                               op0=ALU.mult, op1=ALU.mult, accum_out=stats[t][:, 3:4])
+            else:
+                nc.vector.scalar_tensor_tensor(out=junk[:], in0=work[t][:], scalar=stats[t][:, 1:2],
+                                               in1=x_raw[i][:, j, :], op0=ALU.subtract, op1=ALU.mult,
+                                               accum_out=stats[t][:, 2:3])
+
+        def slope(t):
+            i, j = divmod(t, PACK)
+            if i >= L_GROUPS:
+                nc.vector.tensor_scalar(out=stats[t][:, 3:4], in0=stats[t][:, 2:3],
+                                        scalar1=r2_over_n[:, GROUPS[i], j : j + 1], scalar2=None, op0=ALU.mult)
+
+        def combine(t):
+            i, j = divmod(t, PACK)
+            src = xhat[i, j][:] if i < L_GROUPS else x_raw[i][:, j, :]
+            nc.vector.scalar_tensor_tensor(out=work[t][:], in0=src, scalar=stats[t][:, 3:4], in1=work[t][:],
+                                           op0=ALU.mult, op1=ALU.add, accum_out=stats[t][:, 4:5])
+
+        def finish(t):
+            i, j = divmod(t, PACK)
+            nc.scalar.activation(out=work[t][:], in_=work[t][:], func=IDENT, scale=-float(N), bias=stats[t][:, 4:5])
+            nc.sync.dma_start(out=dx_rows[GROUPS[i]][:, j, :], in_=work[t][:])
+
+        gb_rows = sb.tile([P, P], BF16, name="gb_rows")
+        nc.gpsimd.memset(gb_rows[:], 0.0)
+        ident = sb.tile([P, P], F32, name="ident")
+        make_identity(nc, ident[:])
+        r_pad = sb.tile([P, len(GROUPS), 8], F32, name="r")
+        r = r_pad[:, :, 0:PACK]
+        for c in range(PASSES):
+            cols = slice(c * KP, (c + 1) * KP)
+            tg = sb.tile([P, PACK, KP], BF16, name="g0_%d" % c)
+            nc.sync.dma_start(out=tg[:], in_=g_rows[GROUPS[0]][:, :, cols])
+            g_raw[0, c] = tg[:]
+            if c == 0:
+                nc.scalar.dma_start(out=gb_rows[0:PACK, :], in_=gamma.rearrange("(c p) -> c p", p=P))
+                nc.scalar.dma_start(out=gb_rows[PACK : 2 * PACK, :], in_=beta.rearrange("(c p) -> c p", p=P))
+                nc.scalar.dma_start(out=r, in_=rstd.rearrange("b (g p j) o -> p (b g) (j o)", p=P, j=PACK))
+            tw = sb.tile([P, PACK, KP], BF16, name="w0_%d" % c)
+            nc.sync.dma_start(out=tw[:], in_=weights[0].rearrange("(c p) f -> p c f", p=P)[:, :, cols])
+            w_raw[0, c] = tw[:]
+        load_x(0)
+        load_g(1)
+        load_x(1)
+
+        gb_f32 = sb.tile([P, P], F32, name="gb_f32")
+        nc.scalar.activation(out=gb_f32[:], in_=gb_rows[:], func=IDENT)
+        turn(g_raw[0, 0], ("g", 0, 0))
+        interleave(0, 0, 0, 1, "V")
+        bank = ps.tile([P, N], F32, name="dw", bufs=2)
+        nc.tensor.transpose(bank[:, 0:P], gb_f32[:], ident[:])
+        gb = sb.tile([P, 2 * PACK], F32, name="gb")
+        nc.vector.tensor_copy(out=gb[:], in_=bank[:, 0 : 2 * PACK])
+        r_over_n = sb.tile([P, len(GROUPS), PACK], F32, name="r_over_n")
+        nc.vector.tensor_scalar(out=r_over_n[:], in0=r, scalar1=-1.0 / N, scalar2=None, op0=ALU.mult)
+        quantize_staged(("t", 0, 0))
+        quantize_staged(("g", 0, 0))
+        turn(w_raw[0, 0], ("w", 0, 0))
+        turn(g_raw[0, 1], ("g", 0, 1))
+        interleave(0, 1, 0, 1, "V")
+        quantize_staged(("w", 0, 0))
+        quantize_staged(("g", 0, 1))
+        quantize_staged(("t", 0, 1))
+        turn(w_raw[0, 1], ("w", 0, 1))
+        turn(g_raw[0, 2], ("g", 0, 2))
+        quantize_staged(("w", 0, 1))
+        quantize_staged(("g", 0, 2))
+        turn(w_raw[0, 2], ("w", 0, 2))
+        interleave(0, 2, 0, 1, "V")
+        quantize_staged(("w", 0, 2))
+        r2_over_n = sb.tile([P, len(GROUPS), PACK], F32, name="r2_over_n")
+        nc.vector.tensor_tensor(out=r2_over_n[:], in0=r_over_n[:], in1=r, op=ALU.mult)
+        quantize_staged(("t", 0, 2))
+        bank = ps.tile([P, N], F32, name="dw", bufs=2)
+        for a in range(PACK):
+            nc.tensor.transpose(bank[:, a * P : (a + 1) * P], gb[:, a : a + 1].to_broadcast([P, P]), ident[:])
+        gamma_rows = sb.tile([P, N], F32, name="gamma_rows")
+        nc.scalar.copy(out=gamma_rows[:], in_=bank[:])
+        row_means(0, range(PACK))
+        dh_product(0)
+
+        to_quantize, later, to_store = [], [], []
+
+        def run(item):
+            if item[0] == "U":
+                turn(g_raw[item[1], item[2]], ("g", item[1], item[2]))
+                to_quantize.append(("g", item[1], item[2]))
+            elif item[0] == "W":
+                turn(w_raw[item[1], item[2]], ("w", item[1], item[2]))
+                later.append(("w", item[1], item[2]))
+            elif item[0] == "H":
+                if item[2] == 0:
+                    h_columns(item[1], 0)
+                    h_columns(item[1], 1)
+                elif item[2] == 1:
+                    h_columns(item[1], 2)
+                    h_columns(item[1], 3)
+                    h_rows(item[1], 0)
+                else:
+                    h_rows(item[1], 1)
+                    to_quantize.append(("h", item[1]))
+            elif item[0] == "I":
+                interleave(item[1], item[2], item[3], 2, "S")
+                if item[3] == 1:
+                    later.append(("t", item[1], item[2]))
+            elif item[0] == "J":
+                interleave(item[1], item[2], 0, 1, "V")
+                to_quantize.append(("t", item[1], item[2]))
+            elif item[0] == "O":
+                dw_product(item[1], item[2])
+                to_store.append((item[1], item[2]))
+            elif item[0] == "M":
+                row_means_v(item[1])
+            elif item[0] == "N":
+                row_means(item[1], range(2 * item[2], 2 * item[2] + 2))
+            elif item[0] == "X":
+                normalise(item[1])
+
+        for t in range(STEPS + 3):
+            for kind, k in LOADS.get(t, []):
+                {"g": load_g, "x": load_x, "w": load_w}[kind](k)
+            ready = list(to_quantize)
+            stores = list(to_store)
+            to_quantize.clear()
+            to_quantize.extend(later)
+            later.clear()
+            to_store.clear()
+            items = PLAN.get(t, [])
+            if t < STEPS:
+                scale_rows(t)
+            if t == 0:
+                normalise(0)
+            if t + 1 < STEPS:
+                dh_product(t + 1)
+            if 2 <= t < STEPS + 2:
+                slope(t - 2)
+            if 1 <= t < STEPS + 1:
+                project(t - 1)
+            if t < STEPS:
+                row_mean_d(t)
+            for key in ready[:1]:
+                quantize_staged(key)
+            if 2 <= t < STEPS + 2:
+                combine(t - 2)
+            for key in ready[1:]:
+                quantize_staged(key)
+            lead = 1 if items and items[0][0] != "O" else 0
+            for item in items[:lead]:
+                run(item)
+            if t >= 3:
+                finish(t - 3)
+            for m, c in stores:
+                dw_store(m, c)
+            for item in items[lead:]:
+                run(item)

@@ -4,7 +4,8 @@ import concourse.mybir as mybir
 from concourse.masks import make_identity
 
 T, N, F = 3072, 512, 1536
-FLOPS = 2 * T * N * F + 2 * 1536 * N * F
+T_L = 1536
+FLOPS = 2 * T * N * F + 2 * T_L * N * F
 BYTES = 2 * (T * N + 2 * N + 3 * N * F + T * F) + 4 * (T + T * N + N * F)
 
 F32 = mybir.dt.float32
@@ -14,50 +15,29 @@ U8 = mybir.dt.uint8
 E4M3 = mybir.dt.float8_e4m3fn_x4
 E5M2 = mybir.dt.float8_e5m2_x4
 ALU = mybir.AluOpType
-IDENT = mybir.ActivationFunctionType.Identity
+IDENTITY = mybir.ActivationFunctionType.Identity
 
 P = 128
 PACK = 4
 KP = P * PACK
 PASSES = F // KP
+
 GROUPS = [3, 4, 5, 1, 2, 0]
-L_GROUPS = 3
+WEIGHT_OF = [0, 0, 0, 1, 1, 2]
+L_GROUPS = T_L // KP
+L_STEPS = L_GROUPS * PACK
 STEPS = len(GROUPS) * PACK
 
-PLAN = {
-    0: [("U", 1, 0), ("U", 1, 1), ("H", 0, 0)],
-    1: [("U", 1, 2), ("H", 0, 1), ("M", 1)],
-    2: [("H", 0, 2), ("I", 1, 0, 0), ("I", 1, 0, 1), ("X", 1)],
-    3: [("U", 2, 0), ("H", 1, 0)],
-    4: [("U", 2, 1), ("H", 1, 1)],
-    5: [("U", 2, 2), ("H", 1, 2), ("I", 2, 0, 0), ("M", 2)],
-    6: [("W", 1, 0), ("W", 1, 1), ("X", 2)],
-    7: [("U", 3, 0), ("W", 1, 2)],
-    8: [("U", 3, 1), ("H", 2, 0)],
-    9: [("U", 3, 2), ("H", 2, 1)],
-    10: [("H", 2, 2), ("I", 2, 0, 1), ("I", 1, 1, 0)],
-    11: [("U", 4, 0), ("I", 1, 1, 1)],
-    12: [("U", 4, 1), ("I", 2, 1, 0)],
-    13: [("U", 4, 2), ("I", 2, 1, 1), ("O", 0, 0)],
-    14: [("W", 2, 0), ("W", 2, 1), ("O", 1, 0)],
-    15: [("U", 5, 0), ("W", 2, 2), ("O", 2, 0)],
-    16: [("U", 5, 1), ("I", 1, 2, 0), ("O", 3, 0)],
-    17: [("U", 5, 2), ("I", 1, 2, 1), ("O", 0, 1)],
-    18: [("I", 2, 2, 0), ("I", 2, 2, 1), ("O", 1, 1)],
-    19: [("O", 2, 1), ("O", 3, 1)],
-    21: [("O", 0, 2), ("O", 1, 2)],
-    22: [("O", 2, 2), ("O", 3, 2)],
-}
-LOADS = {0: [("g", 2)], 1: [("x", 2), ("w", 1)], 3: [("g", 3)], 6: [("x", 3)], 7: [("g", 4)],
-         9: [("w", 2)], 10: [("x", 4)], 11: [("g", 5)], 14: [("x", 5)]}
+DH_BANKS, TURN_BANKS = 2, 6
+JOBS_BESIDE_GRAD, JOBS_ALONE = 1, 3
+LOAD_AHEAD = 4
 
 
 def tile_multiscalesattn_pa_v_kernel(
     tc, x, gamma, beta, w_s, b_s, w_m, b_m, w_l, b_l, rstd, grad_out, out_0, out_1
 ):
     nc = tc.nc
-    weights = [w_l, w_m, w_s]
-    weight_of = [0, 0, 0, 1, 1, 2]
+    w_rows = [w.rearrange("(a p) f -> p a f", p=P) for w in (w_l, w_m, w_s)]
     x_rows = x.rearrange("b (g p j) n -> (b g) p j n", p=P, j=PACK)
     g_rows = grad_out.rearrange("b (g p j) f -> (b g) p j f", p=P, j=PACK)
     dx_rows = out_0.rearrange("b (g p j) n -> (b g) p j n", p=P, j=PACK)
@@ -68,313 +48,352 @@ def tile_multiscalesattn_pa_v_kernel(
         ctx.enter_context(tc.manual_schedule())
 
         g_raw, w_raw, x_raw = {}, {}, {}
-        codes = {}
-        xhat, neg_mean, h_t, work, stats, acc = {}, {}, {}, {}, {}, {}
-        staged = {}
+        packed, codes = {}, {}
+        neg_mean, xhat, h_cols = {}, {}, {}
+        dh, rows, stats, raw_sums, dw = {}, {}, {}, {}, {}
+        due = {}
+
+        def load_g_pass(i, c):
+            tile = sb.tile([P, PACK, KP], BF16, name="g_pass%d" % c)
+            nc.sync.dma_start(out=tile[:], in_=g_rows[GROUPS[i]][:, :, c * KP : (c + 1) * KP])
+            g_raw[i, c] = tile[:]
 
         def load_g(i):
-            tag = "g%d" % (i if i < 5 else 3)
-            t = sb.tile([P, PACK, F], BF16, name=tag)
-            nc.sync.dma_start(out=t[:], in_=g_rows[GROUPS[i]])
-            for c in range(PASSES):
-                g_raw[i, c] = t[:, :, c * KP : (c + 1) * KP]
+            if i in (3, 5):
+                for c in range(PASSES):
+                    load_g_pass(i, c)
+            else:
+                tile = sb.tile([P, PACK, F], BF16, name="g_group%d" % i)
+                nc.sync.dma_start(out=tile[:], in_=g_rows[GROUPS[i]])
+                for c in range(PASSES):
+                    g_raw[i, c] = tile[:, :, c * KP : (c + 1) * KP]
 
-        def load_w(k):
-            for c in range(PASSES):
-                t = sb.tile([P, PACK, KP], BF16, name="w0_%d" % c)
-                nc.sync.dma_start(out=t[:], in_=weights[k].rearrange("(c p) f -> p c f", p=P)[:, :, c * KP : (c + 1) * KP])
-                w_raw[k, c] = t[:]
+        def load_w_pass(k, c):
+            tile = sb.tile([P, PACK, KP], BF16, name="w_pass%d" % c)
+            nc.sync.dma_start(out=tile[:], in_=w_rows[k][:, :, c * KP : (c + 1) * KP])
+            w_raw[k, c] = tile[:]
 
         def load_x(i):
-            t = sb.tile([P, PACK, N], BF16, name="x", bufs=3)
-            nc.sync.dma_start(out=t[:], in_=x_rows[GROUPS[i]])
-            x_raw[i] = t
+            x_raw[i] = sb.tile([P, PACK, N], BF16, name="x", bufs=3)
+            nc.sync.dma_start(out=x_raw[i][:], in_=x_rows[GROUPS[i]])
 
-        def turn(src, key):
-            words = src.bitcast(F32)
-            dst = sb.tile([P, PACK, P, 2], F32, name="turned", bufs=5, align_bytes=64)
-            for half in range(2):
-                bank = ps.tile([P, 2, 2, P], F32, name="tbank", bufs=4)
+        def turn_bank():
+            return ps.tile([P, 2, 2, P], F32, name="turn", bufs=TURN_BANKS)
+
+        def pack_from_words(key, tile, halves_of):
+            for first in (0, 2):
+                bank = turn_bank()
                 for a in range(2):
                     for u in range(2):
-                        nc.tensor.transpose(bank[:, a, u, :], words[:, 2 * half + a, u : 2 * P : 2], ident[:])
-                nc.scalar.copy(out=dst[:, 2 * half : 2 * half + 2], in_=bank[:].rearrange("p a u r -> p a r u"))
-            staged[key] = dst[:].rearrange("p a r u -> p (a r u)").bitcast(BF16)
+                        nc.tensor.transpose(bank[:, a, u, :], halves_of(first + a, u), ident[:])
+                nc.scalar.copy(out=tile[:, first : first + 2], in_=bank[:].rearrange("p a u r -> p a r u"))
+            packed[key] = tile[:].rearrange("p a r u -> p (a r u)").bitcast(BF16)
 
-        def quantize(key, fmt, tag, bufs):
-            cw = sb.tile([P, KP], U32, name=tag + "c", bufs=bufs, align_bytes=64)
-            cs = sb.tile([P, KP], U8, name=tag + "s", bufs=bufs, align_bytes=64)
-            nc.vector.quantize_mx(out=cw[:].bitcast(fmt), scales=cs[:], in_=staged[key])
-            codes[key] = (cw, cs)
+        def turn(key, src):
+            words = src.bitcast(F32)
+            tile = sb.tile([P, PACK, P, 2], F32, name="turned", bufs=5, align_bytes=64)
+            pack_from_words(key, tile, lambda a, u: words[:, a, u : 2 * P : 2])
 
-        def quantize_staged(key):
-            if key[0] == "g":
-                quantize(key, E5M2, "gf", 7)
-            elif key[0] == "w":
-                quantize(key, E4M3, "wf", 9)
-            elif key[0] == "t":
-                quantize(key, E5M2, "gt%d_%d" % (key[1], key[2] % 2 if key[1] else key[2]), 1)
-            else:
-                quantize(key, E4M3, "ht", 3)
+        def weave(i, c, part, parts, copy):
+            key = ("g_tokens", i, c)
+            if part == 0:
+                tile = sb.tile([P, KP * PACK], BF16, name="woven", bufs=3, align_bytes=64)
+                packed[key] = tile[:]
+            cols = slice(part * KP // parts, (part + 1) * KP // parts)
+            copy(
+                out=packed[key].rearrange("p (f t) -> p f t", t=PACK)[:, cols].rearrange("p (c i) t -> p c t i", i=4),
+                in_=g_raw[i, c][:, :, cols].rearrange("p t (c i) -> p c t i", i=4),
+            )
 
-        def interleave(i, c, half, halves, engine):
-            key = ("t", i, c)
-            if half == 0:
-                dst = sb.tile([P, KP, PACK], BF16, name="woven", bufs=3, align_bytes=64)
-                work[key] = dst
-                staged[key] = dst[:].rearrange("p f t -> p (f t)")
-            width = KP // halves
-            cols = slice(half * width, (half + 1) * width)
-            src = g_raw[i, c][:, :, cols].rearrange("p t (c i) -> p c t i", i=4)
-            out = work[key][:, cols, :].rearrange("p (c i) t -> p c t i", i=4)
-            if engine == "V":
-                nc.vector.tensor_copy(out=out, in_=src)
-            else:
-                nc.scalar.copy(out=out, in_=src)
+        def quantise(key):
+            fmt, bufs = {
+                "g_features": (E5M2, 2 * PASSES + 1),
+                "w": (E4M3, len(w_rows) * PASSES),
+                "g_tokens": (E5M2, L_GROUPS * PASSES),
+                "h": (E4M3, L_GROUPS),
+            }[key[0]]
+            words = sb.tile([P, KP], U32, name=key[0] + "_codes", bufs=bufs, align_bytes=64)
+            scales = sb.tile([P, KP], U8, name=key[0] + "_scales", bufs=bufs, align_bytes=64)
+            nc.vector.quantize_mx(out=words[:].bitcast(fmt), scales=scales[:], in_=packed[key])
+            codes[key] = (words, scales, fmt)
 
-        def row_means(i, js):
-            if i not in neg_mean:
-                neg_mean[i] = sb.tile([P, PACK], F32, name="negmean", bufs=3)
-            for j in js:
-                junk = sb.tile([P, N], BF16, name="mjunk", bufs=2)
-                nc.scalar.activation(out=junk[:], in_=x_raw[i][:, j, :], func=IDENT, scale=-1.0 / N,
-                                     accum_out=neg_mean[i][:, j : j + 1])
+        def product(bank, stationary, block, moving):
+            cols = slice(block * P, (block + 1) * P)
+            for c in range(PASSES):
+                s_words, s_scales, s_fmt = codes[stationary[c]]
+                m_words, m_scales, m_fmt = codes[moving[c]]
+                nc.tensor.matmul_mx(
+                    out=bank,
+                    lhsT=s_words[:, cols].bitcast(s_fmt),
+                    lhsT_scale=s_scales[:, cols],
+                    rhs=m_words[:].bitcast(m_fmt),
+                    rhs_scale=m_scales[:],
+                    start=(c == 0),
+                    stop=(c == PASSES - 1),
+                )
 
-        def row_means_v(i):
-            neg_mean[i] = sb.tile([P, PACK], F32, name="negmean", bufs=3)
+        def row_means(i, on_vector):
+            neg_mean[i] = sb.tile([P, PACK], F32, name="neg_mean", bufs=L_GROUPS)
             for j in range(PACK):
-                junk = sb.tile([P, N], BF16, name="mjunk", bufs=2)
-                nc.vector.tensor_scalar(out=junk[:], in0=x_raw[i][:, j, :], scalar1=-1.0 / N, scalar2=None,
-                                        op0=ALU.mult, op1=ALU.add, accum_out=neg_mean[i][:, j : j + 1])
+                terms = sb.tile([P, N], BF16, name="mean_terms", bufs=PACK)
+                if on_vector:
+                    nc.vector.tensor_scalar(
+                        out=terms[:], in0=x_raw[i][:, j, :], scalar1=-1.0 / N, scalar2=None,
+                        op0=ALU.mult, op1=ALU.add, accum_out=neg_mean[i][:, j : j + 1],
+                    )
+                else:
+                    nc.scalar.activation(
+                        out=terms[:], in_=x_raw[i][:, j, :], func=IDENTITY, scale=-1.0 / N,
+                        accum_out=neg_mean[i][:, j : j + 1],
+                    )
 
         def normalise(i):
             for j in range(PACK):
-                t = sb.tile([P, N], F32, name="xhat", bufs=8)
-                nc.vector.tensor_scalar(out=t[:], in0=x_raw[i][:, j, :], scalar1=neg_mean[i][:, j : j + 1],
-                                        scalar2=r[:, GROUPS[i], j : j + 1], op0=ALU.add, op1=ALU.mult)
-                xhat[i, j] = t
-
-        def h_columns(i, c):
-            bank = ps.tile([P, 2, 2, P], F32, name="tbank", bufs=4)
-            for j in range(PACK):
-                nc.tensor.transpose(bank[:, j // 2, j % 2, :], xhat[i, j][:, c * P : (c + 1) * P], ident[:])
-            t = sb.tile([P, 2, P, 2], BF16, name="hT", bufs=4)
-            nc.scalar.activation(out=t[:], in_=bank[:].rearrange("n u e p -> n u p e"), func=IDENT,
-                                 scale=gb[:, c : c + 1], bias=gb[:, PACK + c : PACK + c + 1])
-            h_t[i, c] = t[:].rearrange("n u p e -> n u (p e)").bitcast(F32)
-
-        def h_rows(i, half):
-            key = ("h", i)
-            if half == 0:
-                dst = sb.tile([P, PACK, P, 2], F32, name="hrows", bufs=1, align_bytes=64)
-                work[key] = dst
-                staged[key] = dst[:].rearrange("p a r u -> p (a r u)").bitcast(BF16)
-            bank = ps.tile([P, 2, 2, P], F32, name="tbank", bufs=4)
-            for a in range(2):
-                for u in range(2):
-                    nc.tensor.transpose(bank[:, a, u, :], h_t[i, 2 * half + a][:, u, :], ident[:])
-            nc.scalar.copy(out=work[key][:, 2 * half : 2 * half + 2], in_=bank[:].rearrange("p a u r -> p a r u"))
-
-        def product(bank, stat, stat_fmt, cols, mov, mov_fmt):
-            for c in range(PASSES):
-                nc.tensor.matmul_mx(
-                    out=bank[:],
-                    lhsT=stat[c][0][:, cols].bitcast(stat_fmt), lhsT_scale=stat[c][1][:, cols],
-                    rhs=mov[c][0][:].bitcast(mov_fmt), rhs_scale=mov[c][1][:],
-                    start=(c == 0), stop=(c == PASSES - 1),
+                xhat[i, j] = sb.tile([P, N], F32, name="xhat", bufs=2 * PACK)
+                nc.vector.tensor_scalar(
+                    out=xhat[i, j][:], in0=x_raw[i][:, j, :], scalar1=neg_mean[i][:, j : j + 1],
+                    scalar2=r[:, GROUPS[i], j : j + 1], op0=ALU.add, op1=ALU.mult,
                 )
+
+        def h_transposed(i, a):
+            bank = turn_bank()
+            for j in range(PACK):
+                nc.tensor.transpose(bank[:, j // 2, j % 2, :], xhat[i, j][:, a * P : (a + 1) * P], ident[:])
+            tile = sb.tile([P, 2, P, 2], BF16, name="h_cols", bufs=PACK)
+            nc.scalar.activation(
+                out=tile[:], in_=bank[:].rearrange("n u e p -> n u p e"), func=IDENTITY,
+                scale=gamma_beta[:, a : a + 1], bias=gamma_beta[:, PACK + a : PACK + a + 1],
+            )
+            h_cols[i, a] = tile[:].rearrange("n u p e -> n u (p e)").bitcast(F32)
+
+        def uses_raw_x(t):
+            return L_STEPS <= t < STEPS
+
+        def sums_of(t):
+            if t not in raw_sums:
+                raw_sums[t] = sb.tile([P, 4], F32, name="raw_sums", bufs=4)
+            return raw_sums[t]
 
         def dh_product(t):
             i, j = divmod(t, PACK)
-            bank = ps.tile([P, N], F32, name="dh", bufs=2)
-            product(bank, [codes["g", i, c] for c in range(PASSES)], E5M2, slice(j * P, (j + 1) * P),
-                    [codes["w", weight_of[i], c] for c in range(PASSES)], E4M3)
-            acc[t] = bank
+            dh[t] = ps.tile([P, N], F32, name="dh", bufs=DH_BANKS)
+            product(
+                dh[t][:], [("g_features", i, c) for c in range(PASSES)], j,
+                [("w", WEIGHT_OF[i], c) for c in range(PASSES)],
+            )
 
-        def dw_product(m, c):
-            if 2 * c + m // 2 >= 3:
-                bank = ps.tile([P, KP], F32, name="tbank", bufs=4)
-            else:
-                bank = ps.tile([P, KP], F32, name="dw", bufs=2)
-            product(bank, [codes["h", i] for i in range(L_GROUPS)], E4M3, slice(m * P, (m + 1) * P),
-                    [codes["t", i, c] for i in range(L_GROUPS)], E5M2)
-            acc[m, c] = bank
-
-        def dw_store(m, c):
-            t = sb.tile([P, KP], F32, name="dwout", bufs=4)
-            nc.scalar.copy(out=t[:], in_=acc[m, c][:])
-            nc.sync.dma_start(out=out_1[m * P : (m + 1) * P, c * KP : (c + 1) * KP], in_=t[:])
-
-        def scale_rows(t):
+        def scale_dh(t):
             i, j = divmod(t, PACK)
-            work[t] = sb.tile([P, N], F32, name="row", bufs=7)
-            stats[t] = sb.tile([P, 8], F32, name="stats", bufs=7)
-            nc.vector.scalar_tensor_tensor(out=work[t][:], in0=acc[t][:], scalar=r_over_n[:, GROUPS[i], j : j + 1],
-                                           in1=gamma_rows[:], op0=ALU.mult, op1=ALU.mult,
-                                           accum_out=stats[t][:, 0:1] if i >= L_GROUPS else None)
-
-        def row_mean_d(t):
-            if t // PACK >= L_GROUPS:
-                nc.vector.tensor_scalar(out=stats[t][:, 1:2], in0=stats[t][:, 0:1], scalar1=1.0 / N, scalar2=None,
-                                        op0=ALU.mult)
+            rows[t] = sb.tile([P, N], F32, name="rows", bufs=7)
+            stats[t] = sb.tile([P, 2], F32, name="stats", bufs=7)
+            nc.vector.scalar_tensor_tensor(
+                out=rows[t][:], in0=dh[t][:], scalar=neg_r_over_n[:, GROUPS[i], j : j + 1], in1=gamma_rows[:],
+                op0=ALU.mult, op1=ALU.mult, accum_out=sums_of(t)[:, 0:1] if uses_raw_x(t) else None,
+            )
 
         def project(t):
             i, j = divmod(t, PACK)
-            junk = sb.tile([P, N], F32, name="pjunk", bufs=1)
-            if i < L_GROUPS:
-                nc.vector.scalar_tensor_tensor(out=junk[:], in0=work[t][:], scalar=-1.0 / N, in1=xhat[i, j][:],
-                                               op0=ALU.mult, op1=ALU.mult, accum_out=stats[t][:, 3:4])
+            terms = sb.tile([P, N], F32, name="projection_terms", bufs=2)
+            if uses_raw_x(t):
+                nc.vector.scalar_tensor_tensor(
+                    out=terms[:], in0=rows[t][:], scalar=sums_of(t)[:, 2:3], in1=x_raw[i][:, j, :],
+                    op0=ALU.subtract, op1=ALU.mult, accum_out=sums_of(t + 1)[:, 1:2],
+                )
             else:
-                nc.vector.scalar_tensor_tensor(out=junk[:], in0=work[t][:], scalar=stats[t][:, 1:2],
-                                               in1=x_raw[i][:, j, :], op0=ALU.subtract, op1=ALU.mult,
-                                               accum_out=stats[t][:, 2:3])
+                nc.vector.scalar_tensor_tensor(
+                    out=terms[:], in0=rows[t][:], scalar=-1.0 / N, in1=xhat[i, j][:],
+                    op0=ALU.mult, op1=ALU.mult, accum_out=stats[t][:, 0:1],
+                )
 
-        def slope(t):
-            i, j = divmod(t, PACK)
-            if i >= L_GROUPS:
-                nc.vector.tensor_scalar(out=stats[t][:, 3:4], in0=stats[t][:, 2:3],
-                                        scalar1=r2_over_n[:, GROUPS[i], j : j + 1], scalar2=None, op0=ALU.mult)
+        def apply_factors(t):
+            lo = 0 if uses_raw_x(t) else 1
+            hi = 2 if uses_raw_x(t - 1) else 1
+            if lo < hi:
+                i, j = divmod(t - 1, PACK)
+                nc.vector.tensor_tensor(
+                    out=sums_of(t)[:, 2 + lo : 2 + hi], in0=sums_of(t)[:, lo:hi],
+                    in1=factors[:, GROUPS[i], j, lo:hi], op=ALU.mult,
+                )
 
         def combine(t):
             i, j = divmod(t, PACK)
-            src = xhat[i, j][:] if i < L_GROUPS else x_raw[i][:, j, :]
-            nc.vector.scalar_tensor_tensor(out=work[t][:], in0=src, scalar=stats[t][:, 3:4], in1=work[t][:],
-                                           op0=ALU.mult, op1=ALU.add, accum_out=stats[t][:, 4:5])
+            if uses_raw_x(t):
+                z, slope = x_raw[i][:, j, :], sums_of(t + 1)[:, 3:4]
+            else:
+                z, slope = xhat[i, j][:], stats[t][:, 0:1]
+            nc.vector.scalar_tensor_tensor(
+                out=rows[t][:], in0=z, scalar=slope, in1=rows[t][:],
+                op0=ALU.mult, op1=ALU.add, accum_out=stats[t][:, 1:2],
+            )
 
-        def finish(t):
+        def centre_and_store(t):
             i, j = divmod(t, PACK)
-            nc.scalar.activation(out=work[t][:], in_=work[t][:], func=IDENT, scale=-float(N), bias=stats[t][:, 4:5])
-            nc.sync.dma_start(out=dx_rows[GROUPS[i]][:, j, :], in_=work[t][:])
+            if t == STEPS - 1:
+                nc.vector.tensor_scalar(
+                    out=rows[t][:], in0=rows[t][:], scalar1=-float(N), scalar2=stats[t][:, 1:2],
+                    op0=ALU.mult, op1=ALU.add,
+                )
+            else:
+                nc.scalar.activation(
+                    out=rows[t][:], in_=rows[t][:], func=IDENTITY, scale=-float(N), bias=stats[t][:, 1:2]
+                )
+            nc.sync.dma_start(out=dx_rows[GROUPS[i]][:, j, :], in_=rows[t][:])
 
-        gb_rows = sb.tile([P, P], BF16, name="gb_rows")
-        nc.gpsimd.memset(gb_rows[:], 0.0)
+        def dw_product(b):
+            c, a = divmod(b, PACK)
+            dw[b] = turn_bank()[:].rearrange("p a u r -> p (a u r)")
+            product(dw[b], [("h", i) for i in range(L_GROUPS)], a, [("g_tokens", i, c) for i in range(L_GROUPS)])
+
+        def dw_store(b):
+            c, a = divmod(b, PACK)
+            tile = sb.tile([P, KP], F32, name="dw_out", bufs=4)
+            nc.scalar.copy(out=tile[:], in_=dw[b])
+            nc.sync.dma_start(out=out_1[a * P : (a + 1) * P, c * KP : (c + 1) * KP], in_=tile[:])
+
+        def grad_job(i, c, t):
+            turn(("g_features", i, c), g_raw[i, c])
+            due.setdefault(t + 1, []).append(("g_features", i, c))
+
+        def weight_job(k, c, t):
+            turn(("w", k, c), w_raw[k, c])
+            due.setdefault(t + 2, []).append(("w", k, c))
+
+        def h_job(i, part, t):
+            if part < 2:
+                h_transposed(i, 2 * part)
+                h_transposed(i, 2 * part + 1)
+            else:
+                tile = sb.tile([P, PACK, P, 2], F32, name="h_packed", align_bytes=64)
+                pack_from_words(("h", i), tile, lambda a, u: h_cols[i, a][:, u, :])
+                due.setdefault(t + 2, []).append(("h", i))
+
+        def weave_job(ic, part, t):
+            weave(ic[0], ic[1], part, 2, nc.scalar.copy)
+            if part == 1:
+                due.setdefault(t + 2, []).append(("g_tokens", ic[0], ic[1]))
+
+        def h_jobs(i):
+            return [(h_job, i, part) for part in range(3)]
+
+        def weight_jobs(k):
+            return [(weight_job, k, c) for c in range(PASSES)]
+
+        weave_jobs = [(weave_job, (i, c), part) for c in range(PASSES) for i in (1, 2) for part in range(2)]
+        jobs = (
+            h_jobs(0) + weave_jobs[:2] + h_jobs(1) + weight_jobs(1) + h_jobs(2)
+            + weave_jobs[2:8] + weight_jobs(2) + weave_jobs[8:]
+        )
+        grad_jobs = {t: [] for t in range(STEPS + 3)}
+        for i in range(1, len(GROUPS)):
+            for c in range(PASSES):
+                grad_jobs[max(PACK * i - 5 + c, 0)].append((grad_job, i, c))
+        side_jobs, taken = {}, 0
+        for t in range(STEPS + 3):
+            count = JOBS_BESIDE_GRAD if grad_jobs[t] else JOBS_ALONE
+            side_jobs[t] = jobs[taken : taken + count]
+            taken = taken + count
+        last_turn = max(t for t in grad_jobs if grad_jobs[t])
+
+        zero = sb.tile([P, 1], F32, name="zero")
+        nc.vector.memset(zero[:], 0.0)
+        factors = sb.tile([P, len(GROUPS), PACK, 2], F32, name="factors")
+        nc.vector.memset(factors[:], 1.0 / N)
         ident = sb.tile([P, P], F32, name="ident")
         make_identity(nc, ident[:])
-        r_pad = sb.tile([P, len(GROUPS), 8], F32, name="r")
-        r = r_pad[:, :, 0:PACK]
+        square = sb.tile([P, P], BF16, name="square")
+        nc.scalar.activation(out=square[:], in_=zero[:].to_broadcast([P, P]), func=IDENTITY)
+        r_padded = sb.tile([P, len(GROUPS), 8], F32, name="r")
+        r = r_padded[:, :, 0:PACK]
         for c in range(PASSES):
-            cols = slice(c * KP, (c + 1) * KP)
-            tg = sb.tile([P, PACK, KP], BF16, name="g0_%d" % c)
-            nc.sync.dma_start(out=tg[:], in_=g_rows[GROUPS[0]][:, :, cols])
-            g_raw[0, c] = tg[:]
-            if c == 0:
-                nc.scalar.dma_start(out=gb_rows[0:PACK, :], in_=gamma.rearrange("(c p) -> c p", p=P))
-                nc.scalar.dma_start(out=gb_rows[PACK : 2 * PACK, :], in_=beta.rearrange("(c p) -> c p", p=P))
+            load_g_pass(0, c)
+            if c == PASSES - 1:
+                nc.scalar.dma_start(out=square[0:PACK, :], in_=gamma.rearrange("(a p) -> a p", p=P))
+                nc.scalar.dma_start(out=square[PACK : 2 * PACK, :], in_=beta.rearrange("(a p) -> a p", p=P))
                 nc.scalar.dma_start(out=r, in_=rstd.rearrange("b (g p j) o -> p (b g) (j o)", p=P, j=PACK))
-            tw = sb.tile([P, PACK, KP], BF16, name="w0_%d" % c)
-            nc.sync.dma_start(out=tw[:], in_=weights[0].rearrange("(c p) f -> p c f", p=P)[:, :, cols])
-            w_raw[0, c] = tw[:]
+            load_w_pass(0, c)
         load_x(0)
         load_g(1)
         load_x(1)
 
-        gb_f32 = sb.tile([P, P], F32, name="gb_f32")
-        nc.scalar.activation(out=gb_f32[:], in_=gb_rows[:], func=IDENT)
-        turn(g_raw[0, 0], ("g", 0, 0))
-        interleave(0, 0, 0, 1, "V")
-        bank = ps.tile([P, N], F32, name="dw", bufs=2)
-        nc.tensor.transpose(bank[:, 0:P], gb_f32[:], ident[:])
-        gb = sb.tile([P, 2 * PACK], F32, name="gb")
-        nc.vector.tensor_copy(out=gb[:], in_=bank[:, 0 : 2 * PACK])
-        r_over_n = sb.tile([P, len(GROUPS), PACK], F32, name="r_over_n")
-        nc.vector.tensor_scalar(out=r_over_n[:], in0=r, scalar1=-1.0 / N, scalar2=None, op0=ALU.mult)
-        quantize_staged(("t", 0, 0))
-        quantize_staged(("g", 0, 0))
-        turn(w_raw[0, 0], ("w", 0, 0))
-        turn(g_raw[0, 1], ("g", 0, 1))
-        interleave(0, 1, 0, 1, "V")
-        quantize_staged(("w", 0, 0))
-        quantize_staged(("g", 0, 1))
-        quantize_staged(("t", 0, 1))
-        turn(w_raw[0, 1], ("w", 0, 1))
-        turn(g_raw[0, 2], ("g", 0, 2))
-        quantize_staged(("w", 0, 1))
-        quantize_staged(("g", 0, 2))
-        turn(w_raw[0, 2], ("w", 0, 2))
-        interleave(0, 2, 0, 1, "V")
-        quantize_staged(("w", 0, 2))
-        r2_over_n = sb.tile([P, len(GROUPS), PACK], F32, name="r2_over_n")
-        nc.vector.tensor_tensor(out=r2_over_n[:], in0=r_over_n[:], in1=r, op=ALU.mult)
-        quantize_staged(("t", 0, 2))
-        bank = ps.tile([P, N], F32, name="dw", bufs=2)
+        turn(("g_features", 0, 0), g_raw[0, 0])
+        weave(0, 0, 0, 1, nc.vector.tensor_copy)
+        quantise(("g_tokens", 0, 0))
+        quantise(("g_features", 0, 0))
+        turn(("w", 0, 0), w_raw[0, 0])
+        turn(("g_features", 0, 1), g_raw[0, 1])
+        weave(0, 1, 0, 1, nc.vector.tensor_copy)
+        quantise(("w", 0, 0))
+        square_f32 = sb.tile([P, P], F32, name="square_f32")
+        nc.vector.tensor_copy(out=square_f32[:], in_=square[:])
+        quantise(("g_features", 0, 1))
+        quantise(("g_tokens", 0, 1))
+        turn(("w", 0, 1), w_raw[0, 1])
+        columns_bank = ps.tile([P, N], F32, name="dh", bufs=DH_BANKS)
+        nc.tensor.transpose(columns_bank[:, 0:P], square_f32[:], ident[:])
+        turn(("g_features", 0, 2), g_raw[0, 2])
+        quantise(("w", 0, 1))
+        gamma_beta = sb.tile([P, 2 * PACK], F32, name="gamma_beta")
+        nc.vector.tensor_copy(out=gamma_beta[:], in_=columns_bank[:, 0 : 2 * PACK])
+        neg_r_over_n = sb.tile([P, len(GROUPS), PACK], F32, name="neg_r_over_n")
+        nc.vector.tensor_scalar(out=neg_r_over_n[:], in0=r, scalar1=-1.0 / N, scalar2=None, op0=ALU.mult)
+        quantise(("g_features", 0, 2))
+        turn(("w", 0, 2), w_raw[0, 2])
+        weave(0, 2, 0, 1, nc.vector.tensor_copy)
+        quantise(("w", 0, 2))
+        nc.vector.tensor_tensor(out=factors[:, :, :, 1], in0=neg_r_over_n[:], in1=r, op=ALU.mult)
+        quantise(("g_tokens", 0, 2))
+        rows_bank = ps.tile([P, N], F32, name="dh", bufs=DH_BANKS)
         for a in range(PACK):
-            nc.tensor.transpose(bank[:, a * P : (a + 1) * P], gb[:, a : a + 1].to_broadcast([P, P]), ident[:])
+            nc.tensor.transpose(
+                rows_bank[:, a * P : (a + 1) * P], gamma_beta[:, a : a + 1].to_broadcast([P, P]), ident[:]
+            )
         gamma_rows = sb.tile([P, N], F32, name="gamma_rows")
-        nc.scalar.copy(out=gamma_rows[:], in_=bank[:])
-        row_means(0, range(PACK))
+        nc.scalar.copy(out=gamma_rows[:], in_=rows_bank[:])
+        row_means(0, False)
         dh_product(0)
 
-        to_quantize, later, to_store = [], [], []
-
-        def run(item):
-            if item[0] == "U":
-                turn(g_raw[item[1], item[2]], ("g", item[1], item[2]))
-                to_quantize.append(("g", item[1], item[2]))
-            elif item[0] == "W":
-                turn(w_raw[item[1], item[2]], ("w", item[1], item[2]))
-                later.append(("w", item[1], item[2]))
-            elif item[0] == "H":
-                if item[2] == 0:
-                    h_columns(item[1], 0)
-                    h_columns(item[1], 1)
-                elif item[2] == 1:
-                    h_columns(item[1], 2)
-                    h_columns(item[1], 3)
-                    h_rows(item[1], 0)
-                else:
-                    h_rows(item[1], 1)
-                    to_quantize.append(("h", item[1]))
-            elif item[0] == "I":
-                interleave(item[1], item[2], item[3], 2, "S")
-                if item[3] == 1:
-                    later.append(("t", item[1], item[2]))
-            elif item[0] == "J":
-                interleave(item[1], item[2], 0, 1, "V")
-                to_quantize.append(("t", item[1], item[2]))
-            elif item[0] == "O":
-                dw_product(item[1], item[2])
-                to_store.append((item[1], item[2]))
-            elif item[0] == "M":
-                row_means_v(item[1])
-            elif item[0] == "N":
-                row_means(item[1], range(2 * item[2], 2 * item[2] + 2))
-            elif item[0] == "X":
-                normalise(item[1])
-
         for t in range(STEPS + 3):
-            for kind, k in LOADS.get(t, []):
-                {"g": load_g, "x": load_x, "w": load_w}[kind](k)
-            ready = list(to_quantize)
-            stores = list(to_store)
-            to_quantize.clear()
-            to_quantize.extend(later)
-            later.clear()
-            to_store.clear()
-            items = PLAN.get(t, [])
+            for i in range(2, len(GROUPS)):
+                if t == max(PACK * i - 5 - LOAD_AHEAD, 0):
+                    load_g(i)
+                if t == PACK * i - 6:
+                    load_x(i)
+            for job, k, c in side_jobs.get(t + LOAD_AHEAD + 1, []):
+                if job == weight_job:
+                    load_w_pass(k, c)
+
+            ready = due.get(t, [])
             if t < STEPS:
-                scale_rows(t)
-            if t == 0:
-                normalise(0)
+                scale_dh(t)
             if t + 1 < STEPS:
                 dh_product(t + 1)
-            if 2 <= t < STEPS + 2:
-                slope(t - 2)
-            if 1 <= t < STEPS + 1:
+            if 1 <= t <= STEPS:
                 project(t - 1)
-            if t < STEPS:
-                row_mean_d(t)
-            for key in ready[:1]:
-                quantize_staged(key)
-            if 2 <= t < STEPS + 2:
+            for key in ready[:-1]:
+                quantise(key)
+            if 2 <= t <= STEPS + 1:
                 combine(t - 2)
-            for key in ready[1:]:
-                quantize_staged(key)
-            lead = 1 if items and items[0][0] != "O" else 0
-            for item in items[:lead]:
-                run(item)
+            apply_factors(t)
+            for key in ready[-1:]:
+                quantise(key)
+            for i in range(L_GROUPS):
+                if i > 0 and t == PACK * i - 3:
+                    row_means(i, True)
+                if t == max(PACK * i - 2, 0):
+                    normalise(i)
+
+            todo = grad_jobs[t] + side_jobs[t]
+            lead = 1 if todo and todo[0][0] != weave_job else 0
+            for job, first, second in todo[:lead]:
+                job(first, second, t)
             if t >= 3:
-                finish(t - 3)
-            for m, c in stores:
-                dw_store(m, c)
-            for item in items[lead:]:
-                run(item)
+                centre_and_store(t - 3)
+            blocks = range(PASSES * PACK)
+            for b in blocks:
+                if b // 2 == t - 1 - last_turn:
+                    dw_store(b)
+            for b in blocks:
+                if b // 2 == t - last_turn:
+                    dw_product(b)
+            for job, first, second in todo[lead:]:
+                job(first, second, t)

@@ -30,7 +30,7 @@ STEPS = len(GROUPS) * PACK
 
 DH_BANKS, TURN_BANKS = 2, 6
 JOBS_BESIDE_GRAD, JOBS_ALONE = 1, 3
-LOAD_AHEAD = 4
+GRAD_AHEAD, WEIGHT_AHEAD = 4, 5
 
 
 def tile_multiscalesattn_pa_v_kernel(
@@ -91,13 +91,13 @@ def tile_multiscalesattn_pa_v_kernel(
 
         def turn(key, src):
             words = src.bitcast(F32)
-            tile = sb.tile([P, PACK, P, 2], F32, name="turned", bufs=5, align_bytes=64)
+            tile = sb.tile([P, PACK, P, 2], F32, name="turned", bufs=5, align_bytes=256)
             pack_from_words(key, tile, lambda a, u: words[:, a, u : 2 * P : 2])
 
         def weave(i, c, part, parts, copy):
             key = ("g_tokens", i, c)
             if part == 0:
-                tile = sb.tile([P, KP * PACK], BF16, name="woven", bufs=3, align_bytes=64)
+                tile = sb.tile([P, KP * PACK], BF16, name="woven", bufs=3, align_bytes=256)
                 packed[key] = tile[:]
             cols = slice(part * KP // parts, (part + 1) * KP // parts)
             copy(
@@ -112,8 +112,8 @@ def tile_multiscalesattn_pa_v_kernel(
                 "g_tokens": (E5M2, L_GROUPS * PASSES),
                 "h": (E4M3, L_GROUPS),
             }[key[0]]
-            words = sb.tile([P, KP], U32, name=key[0] + "_codes", bufs=bufs, align_bytes=64)
-            scales = sb.tile([P, KP], U8, name=key[0] + "_scales", bufs=bufs, align_bytes=64)
+            words = sb.tile([P, KP], U32, name=key[0] + "_codes", bufs=bufs, align_bytes=256)
+            scales = sb.tile([P, KP], U8, name=key[0] + "_scales", bufs=bufs, align_bytes=256)
             nc.vector.quantize_mx(out=words[:].bitcast(fmt), scales=scales[:], in_=packed[key])
             codes[key] = (words, scales, fmt)
 
@@ -246,7 +246,7 @@ def tile_multiscalesattn_pa_v_kernel(
 
         def dw_store(b):
             c, a = divmod(b, PACK)
-            tile = sb.tile([P, KP], F32, name="dw_out", bufs=4)
+            tile = sb.tile([P, KP], F32, name="dw_out", bufs=6)
             nc.scalar.copy(out=tile[:], in_=dw[b])
             nc.sync.dma_start(out=out_1[a * P : (a + 1) * P, c * KP : (c + 1) * KP], in_=tile[:])
 
@@ -263,7 +263,7 @@ def tile_multiscalesattn_pa_v_kernel(
                 h_transposed(i, 2 * part)
                 h_transposed(i, 2 * part + 1)
             else:
-                tile = sb.tile([P, PACK, P, 2], F32, name="h_packed", align_bytes=64)
+                tile = sb.tile([P, PACK, P, 2], F32, name="h_packed", align_bytes=256)
                 pack_from_words(("h", i), tile, lambda a, u: h_cols[i, a][:, u, :])
                 due.setdefault(t + 2, []).append(("h", i))
 
@@ -354,11 +354,11 @@ def tile_multiscalesattn_pa_v_kernel(
 
         for t in range(STEPS + 3):
             for i in range(2, len(GROUPS)):
-                if t == max(PACK * i - 5 - LOAD_AHEAD, 0):
+                if t == max(PACK * i - 5 - GRAD_AHEAD, 0):
                     load_g(i)
                 if t == PACK * i - 6:
                     load_x(i)
-            for job, k, c in side_jobs.get(t + LOAD_AHEAD + 1, []):
+            for job, k, c in side_jobs.get(t + WEIGHT_AHEAD, []):
                 if job == weight_job:
                     load_w_pass(k, c)
 

from contextlib import ExitStack

import concourse.mybir as mybir
from concourse.masks import make_identity

T, N, F = 3072, 512, 1536
T_L = 1536
FLOPS = 2 * T * N * F + 2 * T_L * N * F
BYTES = 2 * (T * N + 2 * N + 3 * N * F + T * F) + 4 * (T + T * N + N * F)

F32 = mybir.dt.float32
BF16 = mybir.dt.bfloat16
U32 = mybir.dt.uint32
U8 = mybir.dt.uint8
E4M3 = mybir.dt.float8_e4m3fn_x4
E5M2 = mybir.dt.float8_e5m2_x4
ALU = mybir.AluOpType
IDENTITY = mybir.ActivationFunctionType.Identity

P = 128
PACK = 4
KP = P * PACK
PASSES = F // KP

GROUPS = [3, 4, 5, 1, 2, 0]
WEIGHT_OF = [0, 0, 0, 1, 1, 2]
L_GROUPS = T_L // KP
L_STEPS = L_GROUPS * PACK
STEPS = len(GROUPS) * PACK

DH_BANKS, TURN_BANKS = 2, 6
JOBS_BESIDE_GRAD, JOBS_ALONE = 1, 3
GRAD_AHEAD, WEIGHT_AHEAD = 4, 5


def tile_multiscalesattn_pa_v_kernel(
    tc, x, gamma, beta, w_s, b_s, w_m, b_m, w_l, b_l, rstd, grad_out, out_0, out_1
):
    nc = tc.nc
    w_rows = [w.rearrange("(a p) f -> p a f", p=P) for w in (w_l, w_m, w_s)]
    x_rows = x.rearrange("b (g p j) n -> (b g) p j n", p=P, j=PACK)
    g_rows = grad_out.rearrange("b (g p j) f -> (b g) p j f", p=P, j=PACK)
    dx_rows = out_0.rearrange("b (g p j) n -> (b g) p j n", p=P, j=PACK)

    with ExitStack() as ctx:
        sb = ctx.enter_context(tc.tile_pool(name="sb", bufs=1))
        ps = ctx.enter_context(tc.psum_pool(name="ps", bufs=1))
        ctx.enter_context(tc.manual_schedule())

        g_raw, w_raw, x_raw = {}, {}, {}
        packed, codes = {}, {}
        neg_mean, xhat, h_cols = {}, {}, {}
        dh, rows, stats, raw_sums, dw = {}, {}, {}, {}, {}
        due = {}

        def load_g_pass(i, c):
            tile = sb.tile([P, PACK, KP], BF16, name="g_pass%d" % c)
            nc.sync.dma_start(out=tile[:], in_=g_rows[GROUPS[i]][:, :, c * KP : (c + 1) * KP])
            g_raw[i, c] = tile[:]

        def load_g(i):
            if i in (3, 5):
                for c in range(PASSES):
                    load_g_pass(i, c)
            else:
                tile = sb.tile([P, PACK, F], BF16, name="g_group%d" % i)
                nc.sync.dma_start(out=tile[:], in_=g_rows[GROUPS[i]])
                for c in range(PASSES):
                    g_raw[i, c] = tile[:, :, c * KP : (c + 1) * KP]

        def load_w_pass(k, c):
            tile = sb.tile([P, PACK, KP], BF16, name="w_pass%d" % c)
            nc.sync.dma_start(out=tile[:], in_=w_rows[k][:, :, c * KP : (c + 1) * KP])
            w_raw[k, c] = tile[:]

        def load_x(i):
            x_raw[i] = sb.tile([P, PACK, N], BF16, name="x", bufs=3)
            nc.sync.dma_start(out=x_raw[i][:], in_=x_rows[GROUPS[i]])

        def turn_bank():
            return ps.tile([P, 2, 2, P], F32, name="turn", bufs=TURN_BANKS)

        def pack_from_words(key, tile, halves_of):
            for first in (0, 2):
                bank = turn_bank()
                for a in range(2):
                    for u in range(2):
                        nc.tensor.transpose(bank[:, a, u, :], halves_of(first + a, u), ident[:])
                nc.scalar.copy(out=tile[:, first : first + 2], in_=bank[:].rearrange("p a u r -> p a r u"))
            packed[key] = tile[:].rearrange("p a r u -> p (a r u)").bitcast(BF16)

        def turn(key, src):
            words = src.bitcast(F32)
            tile = sb.tile([P, PACK, P, 2], F32, name="turned", bufs=5, align_bytes=256)
            pack_from_words(key, tile, lambda a, u: words[:, a, u : 2 * P : 2])

        def weave(i, c, part, parts, copy):
            key = ("g_tokens", i, c)
            if part == 0:
                tile = sb.tile([P, KP * PACK], BF16, name="woven", bufs=3, align_bytes=256)
                packed[key] = tile[:]
            cols = slice(part * KP // parts, (part + 1) * KP // parts)
            copy(
                out=packed[key].rearrange("p (f t) -> p f t", t=PACK)[:, cols].rearrange("p (c i) t -> p c t i", i=4),
                in_=g_raw[i, c][:, :, cols].rearrange("p t (c i) -> p c t i", i=4),
            )

        def quantise(key):
            fmt, bufs = {
                "g_features": (E5M2, 2 * PASSES + 1),
                "w": (E4M3, len(w_rows) * PASSES),
                "g_tokens": (E5M2, L_GROUPS * PASSES),
                "h": (E4M3, L_GROUPS),
            }[key[0]]
            words = sb.tile([P, KP], U32, name=key[0] + "_codes", bufs=bufs, align_bytes=256)
            scales = sb.tile([P, KP], U8, name=key[0] + "_scales", bufs=bufs, align_bytes=256)
            nc.vector.quantize_mx(out=words[:].bitcast(fmt), scales=scales[:], in_=packed[key])
            codes[key] = (words, scales, fmt)

        def product(bank, stationary, block, moving):
            cols = slice(block * P, (block + 1) * P)
            for c in range(PASSES):
                s_words, s_scales, s_fmt = codes[stationary[c]]
                m_words, m_scales, m_fmt = codes[moving[c]]
                nc.tensor.matmul_mx(
                    out=bank,
                    lhsT=s_words[:, cols].bitcast(s_fmt),
                    lhsT_scale=s_scales[:, cols],
                    rhs=m_words[:].bitcast(m_fmt),
                    rhs_scale=m_scales[:],
                    start=(c == 0),
                    stop=(c == PASSES - 1),
                )

        def row_means(i, on_vector):
            neg_mean[i] = sb.tile([P, PACK], F32, name="neg_mean", bufs=L_GROUPS)
            for j in range(PACK):
                terms = sb.tile([P, N], BF16, name="mean_terms", bufs=PACK)
                if on_vector:
                    nc.vector.tensor_scalar(
                        out=terms[:], in0=x_raw[i][:, j, :], scalar1=-1.0 / N, scalar2=None,
                        op0=ALU.mult, op1=ALU.add, accum_out=neg_mean[i][:, j : j + 1],
                    )
                else:
                    nc.scalar.activation(
                        out=terms[:], in_=x_raw[i][:, j, :], func=IDENTITY, scale=-1.0 / N,
                        accum_out=neg_mean[i][:, j : j + 1],
                    )

        def normalise(i):
            for j in range(PACK):
                xhat[i, j] = sb.tile([P, N], F32, name="xhat", bufs=2 * PACK)
                nc.vector.tensor_scalar(
                    out=xhat[i, j][:], in0=x_raw[i][:, j, :], scalar1=neg_mean[i][:, j : j + 1],
                    scalar2=r[:, GROUPS[i], j : j + 1], op0=ALU.add, op1=ALU.mult,
                )

        def h_transposed(i, a):
            bank = turn_bank()
            for j in range(PACK):
                nc.tensor.transpose(bank[:, j // 2, j % 2, :], xhat[i, j][:, a * P : (a + 1) * P], ident[:])
            tile = sb.tile([P, 2, P, 2], BF16, name="h_cols", bufs=PACK)
            nc.scalar.activation(
                out=tile[:], in_=bank[:].rearrange("n u e p -> n u p e"), func=IDENTITY,
                scale=gamma_beta[:, a : a + 1], bias=gamma_beta[:, PACK + a : PACK + a + 1],
            )
            h_cols[i, a] = tile[:].rearrange("n u p e -> n u (p e)").bitcast(F32)

        def uses_raw_x(t):
            return L_STEPS <= t < STEPS

        def sums_of(t):
            if t not in raw_sums:
                raw_sums[t] = sb.tile([P, 4], F32, name="raw_sums", bufs=4)
            return raw_sums[t]

        def dh_product(t):
            i, j = divmod(t, PACK)
            dh[t] = ps.tile([P, N], F32, name="dh", bufs=DH_BANKS)
            product(
                dh[t][:], [("g_features", i, c) for c in range(PASSES)], j,
                [("w", WEIGHT_OF[i], c) for c in range(PASSES)],
            )

        def scale_dh(t):
            i, j = divmod(t, PACK)
            rows[t] = sb.tile([P, N], F32, name="rows", bufs=7)
            stats[t] = sb.tile([P, 2], F32, name="stats", bufs=7)
            nc.vector.scalar_tensor_tensor(
                out=rows[t][:], in0=dh[t][:], scalar=neg_r_over_n[:, GROUPS[i], j : j + 1], in1=gamma_rows[:],
                op0=ALU.mult, op1=ALU.mult, accum_out=sums_of(t)[:, 0:1] if uses_raw_x(t) else None,
            )

        def project(t):
            i, j = divmod(t, PACK)
            terms = sb.tile([P, N], F32, name="projection_terms", bufs=2)
            if uses_raw_x(t):
                nc.vector.scalar_tensor_tensor(
                    out=terms[:], in0=rows[t][:], scalar=sums_of(t)[:, 2:3], in1=x_raw[i][:, j, :],
                    op0=ALU.subtract, op1=ALU.mult, accum_out=sums_of(t + 1)[:, 1:2],
                )
            else:
                nc.vector.scalar_tensor_tensor(
                    out=terms[:], in0=rows[t][:], scalar=-1.0 / N, in1=xhat[i, j][:],
                    op0=ALU.mult, op1=ALU.mult, accum_out=stats[t][:, 0:1],
                )

        def apply_factors(t):
            lo = 0 if uses_raw_x(t) else 1
            hi = 2 if uses_raw_x(t - 1) else 1
            if lo < hi:
                i, j = divmod(t - 1, PACK)
                nc.vector.tensor_tensor(
                    out=sums_of(t)[:, 2 + lo : 2 + hi], in0=sums_of(t)[:, lo:hi],
                    in1=factors[:, GROUPS[i], j, lo:hi], op=ALU.mult,
                )

        def combine(t):
            i, j = divmod(t, PACK)
            if uses_raw_x(t):
                z, slope = x_raw[i][:, j, :], sums_of(t + 1)[:, 3:4]
            else:
                z, slope = xhat[i, j][:], stats[t][:, 0:1]
            nc.vector.scalar_tensor_tensor(
                out=rows[t][:], in0=z, scalar=slope, in1=rows[t][:],
                op0=ALU.mult, op1=ALU.add, accum_out=stats[t][:, 1:2],
            )

        def centre_and_store(t):
            i, j = divmod(t, PACK)
            if t == STEPS - 1:
                nc.vector.tensor_scalar(
                    out=rows[t][:], in0=rows[t][:], scalar1=-float(N), scalar2=stats[t][:, 1:2],
                    op0=ALU.mult, op1=ALU.add,
                )
            else:
                nc.scalar.activation(
                    out=rows[t][:], in_=rows[t][:], func=IDENTITY, scale=-float(N), bias=stats[t][:, 1:2]
                )
            nc.sync.dma_start(out=dx_rows[GROUPS[i]][:, j, :], in_=rows[t][:])

        def dw_product(b):
            c, a = divmod(b, PACK)
            dw[b] = turn_bank()[:].rearrange("p a u r -> p (a u r)")
            product(dw[b], [("h", i) for i in range(L_GROUPS)], a, [("g_tokens", i, c) for i in range(L_GROUPS)])

        def dw_store(b):
            c, a = divmod(b, PACK)
            tile = sb.tile([P, KP], F32, name="dw_out", bufs=6)
            nc.scalar.copy(out=tile[:], in_=dw[b])
            nc.sync.dma_start(out=out_1[a * P : (a + 1) * P, c * KP : (c + 1) * KP], in_=tile[:])

        def grad_job(i, c, t):
            turn(("g_features", i, c), g_raw[i, c])
            due.setdefault(t + 1, []).append(("g_features", i, c))

        def weight_job(k, c, t):
            turn(("w", k, c), w_raw[k, c])
            due.setdefault(t + 2, []).append(("w", k, c))

        def h_job(i, part, t):
            if part < 2:
                h_transposed(i, 2 * part)
                h_transposed(i, 2 * part + 1)
            else:
                tile = sb.tile([P, PACK, P, 2], F32, name="h_packed", align_bytes=256)
                pack_from_words(("h", i), tile, lambda a, u: h_cols[i, a][:, u, :])
                due.setdefault(t + 2, []).append(("h", i))

        def weave_job(ic, part, t):
            weave(ic[0], ic[1], part, 2, nc.scalar.copy)
            if part == 1:
                due.setdefault(t + 2, []).append(("g_tokens", ic[0], ic[1]))

        def h_jobs(i):
            return [(h_job, i, part) for part in range(3)]

        def weight_jobs(k):
            return [(weight_job, k, c) for c in range(PASSES)]

        weave_jobs = [(weave_job, (i, c), part) for c in range(PASSES) for i in (1, 2) for part in range(2)]
        jobs = (
            h_jobs(0) + weave_jobs[:2] + h_jobs(1) + weight_jobs(1) + h_jobs(2)
            + weave_jobs[2:8] + weight_jobs(2) + weave_jobs[8:]
        )
        grad_jobs = {t: [] for t in range(STEPS + 3)}
        for i in range(1, len(GROUPS)):
            for c in range(PASSES):
                grad_jobs[max(PACK * i - 5 + c, 0)].append((grad_job, i, c))
        side_jobs, taken = {}, 0
        for t in range(STEPS + 3):
            count = JOBS_BESIDE_GRAD if grad_jobs[t] else JOBS_ALONE
            side_jobs[t] = jobs[taken : taken + count]
            taken = taken + count
        last_turn = max(t for t in grad_jobs if grad_jobs[t])

        zero = sb.tile([P, 1], F32, name="zero")
        nc.vector.memset(zero[:], 0.0)
        factors = sb.tile([P, len(GROUPS), PACK, 2], F32, name="factors")
        nc.vector.memset(factors[:], 1.0 / N)
        ident = sb.tile([P, P], F32, name="ident")
        make_identity(nc, ident[:])
        square = sb.tile([P, P], BF16, name="square")
        nc.scalar.activation(out=square[:], in_=zero[:].to_broadcast([P, P]), func=IDENTITY)
        r_padded = sb.tile([P, len(GROUPS), 8], F32, name="r")
        r = r_padded[:, :, 0:PACK]
        for c in range(PASSES):
            load_g_pass(0, c)
            if c == PASSES - 1:
                nc.scalar.dma_start(out=square[0:PACK, :], in_=gamma.rearrange("(a p) -> a p", p=P))
                nc.scalar.dma_start(out=square[PACK : 2 * PACK, :], in_=beta.rearrange("(a p) -> a p", p=P))
                nc.scalar.dma_start(out=r, in_=rstd.rearrange("b (g p j) o -> p (b g) (j o)", p=P, j=PACK))
            load_w_pass(0, c)
        load_x(0)
        load_g(1)
        load_x(1)

        turn(("g_features", 0, 0), g_raw[0, 0])
        weave(0, 0, 0, 1, nc.vector.tensor_copy)
        quantise(("g_tokens", 0, 0))
        quantise(("g_features", 0, 0))
        turn(("w", 0, 0), w_raw[0, 0])
        turn(("g_features", 0, 1), g_raw[0, 1])
        weave(0, 1, 0, 1, nc.vector.tensor_copy)
        quantise(("w", 0, 0))
        square_f32 = sb.tile([P, P], F32, name="square_f32")
        nc.vector.tensor_copy(out=square_f32[:], in_=square[:])
        quantise(("g_features", 0, 1))
        quantise(("g_tokens", 0, 1))
        turn(("w", 0, 1), w_raw[0, 1])
        columns_bank = ps.tile([P, N], F32, name="dh", bufs=DH_BANKS)
        nc.tensor.transpose(columns_bank[:, 0:P], square_f32[:], ident[:])
        turn(("g_features", 0, 2), g_raw[0, 2])
        quantise(("w", 0, 1))
        gamma_beta = sb.tile([P, 2 * PACK], F32, name="gamma_beta")
        nc.vector.tensor_copy(out=gamma_beta[:], in_=columns_bank[:, 0 : 2 * PACK])
        neg_r_over_n = sb.tile([P, len(GROUPS), PACK], F32, name="neg_r_over_n")
        nc.vector.tensor_scalar(out=neg_r_over_n[:], in0=r, scalar1=-1.0 / N, scalar2=None, op0=ALU.mult)
        quantise(("g_features", 0, 2))
        turn(("w", 0, 2), w_raw[0, 2])
        weave(0, 2, 0, 1, nc.vector.tensor_copy)
        quantise(("w", 0, 2))
        nc.vector.tensor_tensor(out=factors[:, :, :, 1], in0=neg_r_over_n[:], in1=r, op=ALU.mult)
        quantise(("g_tokens", 0, 2))
        rows_bank = ps.tile([P, N], F32, name="dh", bufs=DH_BANKS)
        for a in range(PACK):
            nc.tensor.transpose(
                rows_bank[:, a * P : (a + 1) * P], gamma_beta[:, a : a + 1].to_broadcast([P, P]), ident[:]
            )
        gamma_rows = sb.tile([P, N], F32, name="gamma_rows")
        nc.scalar.copy(out=gamma_rows[:], in_=rows_bank[:])
        row_means(0, False)
        dh_product(0)

        for t in range(STEPS + 3):
            for i in range(2, len(GROUPS)):
                if t == max(PACK * i - 5 - GRAD_AHEAD, 0):
                    load_g(i)
                if t == PACK * i - 6:
                    load_x(i)
            for job, k, c in side_jobs.get(t + WEIGHT_AHEAD, []):
                if job == weight_job:
                    load_w_pass(k, c)

            ready = due.get(t, [])
            if t < STEPS:
                scale_dh(t)
            if t + 1 < STEPS:
                dh_product(t + 1)
            if 1 <= t <= STEPS:
                project(t - 1)
            for key in ready[:-1]:
                quantise(key)
            if 2 <= t <= STEPS + 1:
                combine(t - 2)
            apply_factors(t)
            for key in ready[-1:]:
                quantise(key)
            for i in range(L_GROUPS):
                if i > 0 and t == PACK * i - 3:
                    row_means(i, True)
                if t == max(PACK * i - 2, 0):
                    normalise(i)

            todo = grad_jobs[t] + side_jobs[t]
            lead = 1 if todo and todo[0][0] != weave_job else 0
            for job, first, second in todo[:lead]:
                job(first, second, t)
            if t >= 3:
                centre_and_store(t - 3)
            blocks = range(PASSES * PACK)
            for b in blocks:
                if b // 2 == t - 1 - last_turn:
                    dw_store(b)
            for b in blocks:
                if b // 2 == t - last_turn:
                    dw_product(b)
            for job, first, second in todo[lead:]:
                job(first, second, t)
